import numpy as np
import ml_dtypes

BF16 = ml_dtypes.bfloat16


def bf(x):
    return np.asarray(x, np.float32).astype(BF16)


def f32(x):
    return np.asarray(x, np.float32)


def f64(x):
    return np.asarray(x).astype(np.float64)


def striped(idx):
    return np.tile(idx.reshape(-1, 16).T, (8, 1))


C, S, B, T, N = 128, 1024, 256, 8, 2048


def setup_inputs():
    return {"wb": f32(np.random.standard_normal((C, S)) / np.sqrt(T)), "wout": bf(np.random.standard_normal((C, S)) / np.sqrt(C)), "offs": striped(np.random.permutation(np.tile(np.arange(S), 2))[:N])}


def reference(wb, wout, offs):
    idx = offs[:16].T.reshape(-1)
    u = f64(wb)[:, idx].reshape(C, T, B).sum(axis=1)
    z = u.T @ f64(wout)
    m = z.max(axis=1, keepdims=True)
    return z - m - np.log(np.exp(z - m).sum(axis=1, keepdims=True))

@@ -1,0 +1,74 @@
+import concourse.mybir as mybir
+
+F32 = mybir.dt.float32
+BF16 = mybir.dt.bfloat16
+U16 = mybir.dt.uint16
+ADD = mybir.AluOpType.add
+SUBTRACT = mybir.AluOpType.subtract
+MAX = mybir.AluOpType.max
+EXP = mybir.ActivationFunctionType.Exp
+LN = mybir.ActivationFunctionType.Ln
+X = mybir.AxisListType.X
+
+C = 128
+S = 1024
+B = 256
+T = 8
+N = T * B
+P = 128
+BANK = 512
+PER_COLUMN = 16
+
+FLOPS = 2 * B * C * S
+
+
+def tile_gmemn2n_kernel(tc, wb, wout, offs, out):
+    nc = tc.nc
+    with (
+        tc.tile_pool(name="held", bufs=1) as held,
+        tc.tile_pool(name="work", bufs=2) as work,
+        tc.psum_pool(name="psum", bufs=2) as psum,
+    ):
+        offsets = held.tile([P, N // PER_COLUMN], U16, name="offsets")
+        nc.sync.dma_start(offsets[:], offs)
+        table = held.tile([C, S], F32, name="table")
+        nc.scalar.dma_start(table[:], wb)
+        answers = held.tile([C, S], BF16, name="answers")
+        nc.gpsimd.dma_start(answers[:], wout)
+
+        u = work.tile([C, B], F32, name="u")
+        nc.vector.memset(u[:], 0.0)
+        piece = B // PER_COLUMN
+        for t in range(T):
+            words = table[:].indirect(offsets[:, t * piece : (t + 1) * piece])
+            longer = work.tile([C, B], F32, name="u")
+            nc.vector.tensor_tensor(longer[:], words, u[:], ADD)
+            u = longer
+        u_bf = held.tile([C, B], BF16, name="u_bf")
+        nc.vector.tensor_copy(u_bf[:], u[:])
+
+        for q in range(B // P):
+            halves = [slice(h * BANK, (h + 1) * BANK) for h in range(S // BANK)]
+            z = psum.tile([P, S], F32, name="z")
+            for half in halves:
+                nc.tensor.matmul(z[:, half], u_bf[:, q * P : (q + 1) * P], answers[:, half], start=True, stop=True)
+
+            peaks = work.tile([P, len(halves)], F32, name="peaks")
+            for h, half in enumerate(halves):
+                nc.vector.reduce_max(peaks[:, h : h + 1], z[:, half], axis=X)
+            minus_peak = work.tile([P, 1], F32, name="minus_peak")
+            nc.vector.tensor_reduce(minus_peak[:], peaks[:], axis=X, op=MAX, negate=True)
+
+            sums = work.tile([P, len(halves)], F32, name="sums")
+            powers = work.tile([P, S], BF16, name="powers")
+            for h, half in enumerate(halves):
+                nc.scalar.activation(
+                    powers[:, half], z[:, half], EXP, bias=minus_peak[:], accum_out=sums[:, h : h + 1]
+                )
+            log_sum = work.tile([P, 1], F32, name="log_sum")
+            nc.scalar.activation(log_sum[:], sums[:, 0:1], LN, bias=sums[:, 1:2])
+
+            result = work.tile([P, S], F32, name="result")
+            for half in halves:
+                nc.vector.tensor_scalar(result[:, half], z[:, half], minus_peak[:], log_sum[:], op0=ADD, op1=SUBTRACT)
+            nc.sync.dma_start(out[q * P : (q + 1) * P, :], result[:])

@@ -8,6 +8,7 @@ SUBTRACT = mybir.AluOpType.subtract
 MAX = mybir.AluOpType.max
 EXP = mybir.ActivationFunctionType.Exp
 LN = mybir.ActivationFunctionType.Ln
+IDENTITY = mybir.ActivationFunctionType.Identity
 X = mybir.AxisListType.X
 
 C = 128
@@ -24,6 +25,7 @@ FLOPS = 2 * B * C * S
 
 def tile_gmemn2n_kernel(tc, wb, wout, offs, out):
     nc = tc.nc
+    low, high = slice(0, BANK), slice(BANK, S)
     with (
         tc.tile_pool(name="held", bufs=1) as held,
         tc.tile_pool(name="work", bufs=2) as work,
@@ -32,43 +34,47 @@ def tile_gmemn2n_kernel(tc, wb, wout, offs, out):
         offsets = held.tile([P, N // PER_COLUMN], U16, name="offsets")
         nc.sync.dma_start(offsets[:], offs)
         table = held.tile([C, S], F32, name="table")
-        nc.scalar.dma_start(table[:], wb)
+        nc.scalar.dma_start(table[:, high], wb[:, high])
+        nc.sync.dma_start(table[:, low], wb[:, low])
         answers = held.tile([C, S], BF16, name="answers")
-        nc.gpsimd.dma_start(answers[:], wout)
-
-        u = work.tile([C, B], F32, name="u")
-        nc.vector.memset(u[:], 0.0)
-        piece = B // PER_COLUMN
-        for t in range(T):
-            words = table[:].indirect(offsets[:, t * piece : (t + 1) * piece])
-            longer = work.tile([C, B], F32, name="u")
-            nc.vector.tensor_tensor(longer[:], words, u[:], ADD)
-            u = longer
-        u_bf = held.tile([C, B], BF16, name="u_bf")
-        nc.vector.tensor_copy(u_bf[:], u[:])
+        nc.scalar.dma_start(answers[:], wout)
+        zeros = held.tile([C, P], F32, name="zeros")
+        nc.vector.memset(zeros[:], 0.0)
 
         for q in range(B // P):
-            halves = [slice(h * BANK, (h + 1) * BANK) for h in range(S // BANK)]
-            z = psum.tile([P, S], F32, name="z")
-            for half in halves:
-                nc.tensor.matmul(z[:, half], u_bf[:, q * P : (q + 1) * P], answers[:, half], start=True, stop=True)
+            bags = [zeros, zeros]
+            for t in range(T):
+                first = (t * B + q * P) // PER_COLUMN
+                words = table[:].indirect(offsets[:, first : first + P // PER_COLUMN])
+                longer = work.tile([C, P], F32, name=f"bag{t % 2}")
+                nc.vector.tensor_tensor(longer[:], words, bags[t % 2][:], ADD)
+                bags[t % 2] = longer
+            u_bf = work.tile([C, P], BF16, name="u_bf")
+            nc.vector.tensor_tensor(u_bf[:], bags[0][:], bags[1][:], ADD)
 
-            peaks = work.tile([P, len(halves)], F32, name="peaks")
-            for h, half in enumerate(halves):
-                nc.vector.reduce_max(peaks[:, h : h + 1], z[:, half], axis=X)
+            z = psum.tile([P, S], F32, name="z")
+            for half in (low, high):
+                nc.tensor.matmul(z[:, half], u_bf[:], answers[:, half], start=True, stop=True)
+
+            peaks = work.tile([P, 2], F32, name="peaks")
+            nc.vector.reduce_max(peaks[:, 0:1], z[:, low], axis=X)
+            nc.vector.reduce_max(peaks[:, 1:2], z[:, high], axis=X)
             minus_peak = work.tile([P, 1], F32, name="minus_peak")
             nc.vector.tensor_reduce(minus_peak[:], peaks[:], axis=X, op=MAX, negate=True)
 
-            sums = work.tile([P, len(halves)], F32, name="sums")
+            sums = work.tile([P, 2], F32, name="sums")
             powers = work.tile([P, S], BF16, name="powers")
-            for h, half in enumerate(halves):
-                nc.scalar.activation(
-                    powers[:, half], z[:, half], EXP, bias=minus_peak[:], accum_out=sums[:, h : h + 1]
-                )
+            nc.scalar.activation(powers[:, low], z[:, low], EXP, bias=minus_peak[:], accum_out=sums[:, 0:1])
+            nc.scalar.activation(powers[:, high], z[:, high], EXP, bias=minus_peak[:], accum_out=sums[:, 1:2])
             log_sum = work.tile([P, 1], F32, name="log_sum")
             nc.scalar.activation(log_sum[:], sums[:, 0:1], LN, bias=sums[:, 1:2])
 
-            result = work.tile([P, S], F32, name="result")
-            for half in halves:
-                nc.vector.tensor_scalar(result[:, half], z[:, half], minus_peak[:], log_sum[:], op0=ADD, op1=SUBTRACT)
-            nc.sync.dma_start(out[q * P : (q + 1) * P, :], result[:])
+            rows = slice(q * P, (q + 1) * P)
+            result_low = work.tile([P, BANK], F32, name="result_low")
+            nc.vector.tensor_scalar(result_low[:], z[:, low], minus_peak[:], log_sum[:], op0=ADD, op1=SUBTRACT)
+            nc.sync.dma_start(out[rows, low], result_low[:])
+            shift = work.tile([P, 1], F32, name="shift")
+            nc.scalar.activation(shift[:], log_sum[:], IDENTITY, bias=minus_peak[:], scale=-1.0)
+            result_high = work.tile([P, BANK], F32, name="result_high")
+            nc.scalar.activation(result_high[:], z[:, high], IDENTITY, bias=shift[:])
+            nc.scalar.dma_start(out[rows, high], result_high[:])

@@ -5,11 +5,10 @@ BF16 = mybir.dt.bfloat16
 U16 = mybir.dt.uint16
 ADD = mybir.AluOpType.add
 SUBTRACT = mybir.AluOpType.subtract
-MAX = mybir.AluOpType.max
+MULT = mybir.AluOpType.mult
+MIN = mybir.AluOpType.min
 EXP = mybir.ActivationFunctionType.Exp
 LN = mybir.ActivationFunctionType.Ln
-IDENTITY = mybir.ActivationFunctionType.Identity
-X = mybir.AxisListType.X
 
 C = 128
 S = 1024
@@ -26,10 +25,11 @@ FLOPS = 2 * B * C * S
 def tile_gmemn2n_kernel(tc, wb, wout, offs, out):
     nc = tc.nc
     low, high = slice(0, BANK), slice(BANK, S)
+    blocks = range(B // P)
     with (
         tc.tile_pool(name="held", bufs=1) as held,
         tc.tile_pool(name="work", bufs=2) as work,
-        tc.psum_pool(name="psum", bufs=2) as psum,
+        tc.psum_pool(name="psum", bufs=1) as psum,
     ):
         offsets = held.tile([P, N // PER_COLUMN], U16, name="offsets")
         nc.sync.dma_start(offsets[:], offs)
@@ -41,7 +41,8 @@ def tile_gmemn2n_kernel(tc, wb, wout, offs, out):
         zeros = held.tile([C, P], F32, name="zeros")
         nc.vector.memset(zeros[:], 0.0)
 
-        for q in range(B // P):
+        z = []
+        for q in blocks:
             bags = [zeros, zeros]
             for t in range(T):
                 first = (t * B + q * P) // PER_COLUMN
@@ -51,30 +52,31 @@ def tile_gmemn2n_kernel(tc, wb, wout, offs, out):
                 bags[t % 2] = longer
             u_bf = work.tile([C, P], BF16, name="u_bf")
             nc.vector.tensor_tensor(u_bf[:], bags[0][:], bags[1][:], ADD)
-
-            z = psum.tile([P, S], F32, name="z")
+            z.append(psum.tile([P, S], F32, name=f"z{q}"))
             for half in (low, high):
-                nc.tensor.matmul(z[:, half], u_bf[:], answers[:, half], start=True, stop=True)
+                nc.tensor.matmul(z[q][:, half], u_bf[:], answers[:, half], start=True, stop=True)
 
-            peaks = work.tile([P, 2], F32, name="peaks")
-            nc.vector.reduce_max(peaks[:, 0:1], z[:, low], axis=X)
-            nc.vector.reduce_max(peaks[:, 1:2], z[:, high], axis=X)
-            minus_peak = work.tile([P, 1], F32, name="minus_peak")
-            nc.vector.tensor_reduce(minus_peak[:], peaks[:], axis=X, op=MAX, negate=True)
-
-            sums = work.tile([P, 2], F32, name="sums")
+        minus_z = [held.tile([P, S], F32, name=f"minus_z{q}") for q in blocks]
+        minus_peaks = held.tile([P, len(blocks)], F32, name="minus_peaks")
+        totals = held.tile([P, len(blocks)], F32, name="totals")
+        for q in blocks:
+            minus_peak = minus_peaks[:, q : q + 1]
+            of_low = work.tile([P, 1], F32, name="of_low")
+            nc.vector.tensor_scalar(minus_z[q][:, low], z[q][:, low], -1.0, None, op0=MULT, op1=MIN, accum_out=of_low[:])
+            nc.vector.tensor_scalar(
+                minus_z[q][:, high], z[q][:, high], -1.0, of_low[:], op0=MULT, op1=MIN, accum_out=minus_peak
+            )
             powers = work.tile([P, S], BF16, name="powers")
-            nc.scalar.activation(powers[:, low], z[:, low], EXP, bias=minus_peak[:], accum_out=sums[:, 0:1])
-            nc.scalar.activation(powers[:, high], z[:, high], EXP, bias=minus_peak[:], accum_out=sums[:, 1:2])
-            log_sum = work.tile([P, 1], F32, name="log_sum")
-            nc.scalar.activation(log_sum[:], sums[:, 0:1], LN, bias=sums[:, 1:2])
+            nc.scalar.activation(
+                powers[:], minus_z[q][:], EXP, bias=minus_peak, scale=-1.0, accum_out=totals[:, q : q + 1]
+            )
 
-            rows = slice(q * P, (q + 1) * P)
-            result_low = work.tile([P, BANK], F32, name="result_low")
-            nc.vector.tensor_scalar(result_low[:], z[:, low], minus_peak[:], log_sum[:], op0=ADD, op1=SUBTRACT)
-            nc.sync.dma_start(out[rows, low], result_low[:])
-            shift = work.tile([P, 1], F32, name="shift")
-            nc.scalar.activation(shift[:], log_sum[:], IDENTITY, bias=minus_peak[:], scale=-1.0)
-            result_high = work.tile([P, BANK], F32, name="result_high")
-            nc.scalar.activation(result_high[:], z[:, high], IDENTITY, bias=shift[:])
-            nc.scalar.dma_start(out[rows, high], result_high[:])
+        log_sums = held.tile([P, len(blocks)], F32, name="log_sums")
+        nc.scalar.activation(log_sums[:], totals[:], LN)
+        shifts = held.tile([P, len(blocks)], F32, name="shifts")
+        nc.vector.tensor_tensor(shifts[:], minus_peaks[:], log_sums[:], SUBTRACT)
+        for q in blocks:
+            for half, queue in ((low, nc.sync), (high, nc.scalar)):
+                result = work.tile([P, BANK], F32, name="result")
+                nc.vector.tensor_scalar(result[:], minus_z[q][:, half], -1.0, shifts[:, q : q + 1], op0=MULT, op1=ADD)
+                queue.dma_start(out[q * P : (q + 1) * P, half], result[:])

@@ -71,12 +71,14 @@ def tile_gmemn2n_kernel(tc, wb, wout, offs, out):
                 powers[:], minus_z[q][:], EXP, bias=minus_peak, scale=-1.0, accum_out=totals[:, q : q + 1]
             )
 
+        centred = [held.tile([P, S], F32, name=f"centred{q}") for q in blocks]
+        for q in blocks:
+            nc.vector.tensor_scalar(centred[q][:], minus_z[q][:], -1.0, minus_peaks[:, q : q + 1], op0=MULT, op1=ADD)
+
         log_sums = held.tile([P, len(blocks)], F32, name="log_sums")
         nc.scalar.activation(log_sums[:], totals[:], LN)
-        shifts = held.tile([P, len(blocks)], F32, name="shifts")
-        nc.vector.tensor_tensor(shifts[:], minus_peaks[:], log_sums[:], SUBTRACT)
         for q in blocks:
-            for half, queue in ((low, nc.sync), (high, nc.scalar)):
-                result = work.tile([P, BANK], F32, name="result")
-                nc.vector.tensor_scalar(result[:], minus_z[q][:, half], -1.0, shifts[:, q : q + 1], op0=MULT, op1=ADD)
+            for h, (half, queue) in enumerate(((low, nc.sync), (high, nc.scalar))):
+                result = held.tile([P, BANK], F32, name=f"result{q}{h}")
+                nc.vector.tensor_scalar(result[:], centred[q][:, half], log_sums[:, q : q + 1], None, op0=SUBTRACT)
                 queue.dma_start(out[q * P : (q + 1) * P, half], result[:])

@@ -1,3 +1,5 @@
+import math
+
 import concourse.mybir as mybir
 
 F32 = mybir.dt.float32
@@ -5,10 +7,10 @@ BF16 = mybir.dt.bfloat16
 U16 = mybir.dt.uint16
 ADD = mybir.AluOpType.add
 SUBTRACT = mybir.AluOpType.subtract
+IS_LE = mybir.AluOpType.is_le
 MULT = mybir.AluOpType.mult
 MIN = mybir.AluOpType.min
 EXP = mybir.ActivationFunctionType.Exp
-LN = mybir.ActivationFunctionType.Ln
 
 C = 128
 S = 1024
@@ -18,6 +20,8 @@ N = T * B
 P = 128
 BANK = 512
 PER_COLUMN = 16
+RUNGS = 256
+STEP = math.log(S) / RUNGS
 
 FLOPS = 2 * B * C * S
 
@@ -41,6 +45,12 @@ def tile_gmemn2n_kernel(tc, wb, wout, offs, out):
         zeros = held.tile([C, P], F32, name="zeros")
         nc.vector.memset(zeros[:], 0.0)
 
+        minus_one = held.tile([P, 1], F32, name="minus_one")
+        nc.vector.memset(minus_one[:], -1.0)
+        ladder = held.tile([P, RUNGS], F32, name="ladder")
+        nc.gpsimd.iota(ladder[:], [[1, RUNGS]], base=1, channel_multiplier=0, allow_small_or_imprecise_dtypes=True)
+        nc.scalar.activation(ladder[:], ladder[:], EXP, scale=STEP)
+
         z = []
         for q in blocks:
             bags = [zeros, zeros]
@@ -56,29 +66,31 @@ def tile_gmemn2n_kernel(tc, wb, wout, offs, out):
             for half in (low, high):
                 nc.tensor.matmul(z[q][:, half], u_bf[:], answers[:, half], start=True, stop=True)
 
-        minus_z = [held.tile([P, S], F32, name=f"minus_z{q}") for q in blocks]
-        minus_peaks = held.tile([P, len(blocks)], F32, name="minus_peaks")
-        totals = held.tile([P, len(blocks)], F32, name="totals")
         for q in blocks:
-            minus_peak = minus_peaks[:, q : q + 1]
+            minus_z = work.tile([P, S], F32, name="minus_z")
             of_low = work.tile([P, 1], F32, name="of_low")
-            nc.vector.tensor_scalar(minus_z[q][:, low], z[q][:, low], -1.0, None, op0=MULT, op1=MIN, accum_out=of_low[:])
+            minus_peak = work.tile([P, 1], F32, name="minus_peak")
+            nc.vector.tensor_scalar(minus_z[:, low], z[q][:, low], -1.0, None, op0=MULT, op1=MIN, accum_out=of_low[:])
             nc.vector.tensor_scalar(
-                minus_z[q][:, high], z[q][:, high], -1.0, of_low[:], op0=MULT, op1=MIN, accum_out=minus_peak
+                minus_z[:, high], z[q][:, high], -1.0, of_low[:], op0=MULT, op1=MIN, accum_out=minus_peak[:]
             )
             powers = work.tile([P, S], BF16, name="powers")
-            nc.scalar.activation(
-                powers[:], minus_z[q][:], EXP, bias=minus_peak, scale=-1.0, accum_out=totals[:, q : q + 1]
+            total = work.tile([P, 1], F32, name="total")
+            nc.scalar.activation(powers[:], minus_z[:], EXP, bias=minus_peak[:], scale=-1.0, accum_out=total[:])
+
+            below = work.tile([P, RUNGS], F32, name="below")
+            rungs_below = work.tile([P, 1], F32, name="rungs_below")
+            nc.vector.tensor_scalar(
+                below[:], ladder[:], total[:], 0.5 - 1.0 / STEP, op0=IS_LE, op1=ADD, accum_out=rungs_below[:]
             )
+            shrink = work.tile([P, 1], F32, name="shrink")
+            nc.scalar.activation(shrink[:], rungs_below[:], EXP, bias=minus_one[:], scale=-STEP)
+            rest = work.tile([P, 1], F32, name="rest")
+            nc.vector.tensor_scalar(rest[:], rungs_below[:], STEP, minus_peak[:], op0=MULT, op1=SUBTRACT)
+            log_sum_exp = work.tile([P, 1], F32, name="log_sum_exp")
+            nc.vector.tensor_scalar(log_sum_exp[:], shrink[:], total[:], rest[:], op0=MULT, op1=ADD)
 
-        centred = [held.tile([P, S], F32, name=f"centred{q}") for q in blocks]
-        for q in blocks:
-            nc.vector.tensor_scalar(centred[q][:], minus_z[q][:], -1.0, minus_peaks[:, q : q + 1], op0=MULT, op1=ADD)
-
-        log_sums = held.tile([P, len(blocks)], F32, name="log_sums")
-        nc.scalar.activation(log_sums[:], totals[:], LN)
-        for q in blocks:
             for h, (half, queue) in enumerate(((low, nc.sync), (high, nc.scalar))):
                 result = held.tile([P, BANK], F32, name=f"result{q}{h}")
-                nc.vector.tensor_scalar(result[:], centred[q][:, half], log_sums[:, q : q + 1], None, op0=SUBTRACT)
+                nc.vector.tensor_scalar(result[:], minus_z[:, half], log_sum_exp[:], -1.0, op0=ADD, op1=MULT)
                 queue.dma_start(out[q * P : (q + 1) * P, half], result[:])

@@ -42,7 +42,7 @@ def tile_gmemn2n_kernel(tc, wb, wout, offs, out):
         nc.sync.dma_start(table[:, low], wb[:, low])
         answers = held.tile([C, S], BF16, name="answers")
         nc.scalar.dma_start(answers[:], wout)
-        zeros = held.tile([C, P], F32, name="zeros")
+        zeros = held.tile([C, B], F32, name="zeros")
         nc.vector.memset(zeros[:], 0.0)
 
         minus_one = held.tile([P, 1], F32, name="minus_one")
@@ -51,17 +51,18 @@ def tile_gmemn2n_kernel(tc, wb, wout, offs, out):
         nc.gpsimd.iota(ladder[:], [[1, RUNGS]], base=1, channel_multiplier=0, allow_small_or_imprecise_dtypes=True)
         nc.scalar.activation(ladder[:], ladder[:], EXP, scale=STEP)
 
+        bags = [zeros, zeros]
+        for t in range(T):
+            words = table[:].indirect(offsets[:, t * B // PER_COLUMN : (t + 1) * B // PER_COLUMN])
+            longer = work.tile([C, B], F32, name=f"bag{t % 2}")
+            nc.vector.tensor_tensor(longer[:], words, bags[t % 2][:], ADD)
+            bags[t % 2] = longer
+
         z = []
         for q in blocks:
-            bags = [zeros, zeros]
-            for t in range(T):
-                first = (t * B + q * P) // PER_COLUMN
-                words = table[:].indirect(offsets[:, first : first + P // PER_COLUMN])
-                longer = work.tile([C, P], F32, name=f"bag{t % 2}")
-                nc.vector.tensor_tensor(longer[:], words, bags[t % 2][:], ADD)
-                bags[t % 2] = longer
+            asked = slice(q * P, (q + 1) * P)
             u_bf = work.tile([C, P], BF16, name="u_bf")
-            nc.vector.tensor_tensor(u_bf[:], bags[0][:], bags[1][:], ADD)
+            nc.vector.tensor_tensor(u_bf[:], bags[0][:, asked], bags[1][:, asked], ADD)
             z.append(psum.tile([P, S], F32, name=f"z{q}"))
             for half in (low, high):
                 nc.tensor.matmul(z[q][:, half], u_bf[:], answers[:, half], start=True, stop=True)

@@ -52,7 +52,7 @@ def tile_gmemn2n_kernel(tc, wb, wout, offs, out):
         nc.scalar.activation(ladder[:], ladder[:], EXP, scale=STEP)
 
         bags = [zeros, zeros]
-        for t in range(T):
+        for t in range(T // 2):
             words = table[:].indirect(offsets[:, t * B // PER_COLUMN : (t + 1) * B // PER_COLUMN])
             longer = work.tile([C, B], F32, name=f"bag{t % 2}")
             nc.vector.tensor_tensor(longer[:], words, bags[t % 2][:], ADD)
@@ -61,8 +61,15 @@ def tile_gmemn2n_kernel(tc, wb, wout, offs, out):
         z = []
         for q in blocks:
             asked = slice(q * P, (q + 1) * P)
+            mine = [bags[0][:, asked], bags[1][:, asked]]
+            for t in range(T // 2, T):
+                first = (t * B + q * P) // PER_COLUMN
+                words = table[:].indirect(offsets[:, first : first + P // PER_COLUMN])
+                longer = work.tile([C, P], F32, name=f"mine{t % 2}")
+                nc.vector.tensor_tensor(longer[:], words, mine[t % 2], ADD)
+                mine[t % 2] = longer[:]
             u_bf = work.tile([C, P], BF16, name="u_bf")
-            nc.vector.tensor_tensor(u_bf[:], bags[0][:, asked], bags[1][:, asked], ADD)
+            nc.vector.tensor_tensor(u_bf[:], mine[0], mine[1], ADD)
             z.append(psum.tile([P, S], F32, name=f"z{q}"))
             for half in (low, high):
                 nc.tensor.matmul(z[q][:, half], u_bf[:], answers[:, half], start=True, stop=True)

@@ -7,7 +7,6 @@ BF16 = mybir.dt.bfloat16
 U16 = mybir.dt.uint16
 ADD = mybir.AluOpType.add
 SUBTRACT = mybir.AluOpType.subtract
-IS_LE = mybir.AluOpType.is_le
 MULT = mybir.AluOpType.mult
 MIN = mybir.AluOpType.min
 EXP = mybir.ActivationFunctionType.Exp
@@ -22,6 +21,9 @@ BANK = 512
 PER_COLUMN = 16
 RUNGS = 256
 STEP = math.log(S) / RUNGS
+FIRST_SLOPE = STEP / (math.exp(STEP) - 1.0)
+LAST_SLOPE = FIRST_SLOPE * math.exp(-(RUNGS - 1) * STEP)
+SAG = STEP * STEP / 16.0
 
 FLOPS = 2 * B * C * S
 
@@ -45,11 +47,15 @@ def tile_gmemn2n_kernel(tc, wb, wout, offs, out):
         zeros = held.tile([C, B], F32, name="zeros")
         nc.vector.memset(zeros[:], 0.0)
 
-        minus_one = held.tile([P, 1], F32, name="minus_one")
-        nc.vector.memset(minus_one[:], -1.0)
-        ladder = held.tile([P, RUNGS], F32, name="ladder")
-        nc.gpsimd.iota(ladder[:], [[1, RUNGS]], base=1, channel_multiplier=0, allow_small_or_imprecise_dtypes=True)
-        nc.scalar.activation(ladder[:], ladder[:], EXP, scale=STEP)
+        count = held.tile([P, RUNGS], F32, name="count")
+        nc.gpsimd.iota(count[:], [[1, RUNGS]], base=1, channel_multiplier=0, allow_small_or_imprecise_dtypes=True)
+        ln_step = held.tile([P, 1], F32, name="ln_step")
+        nc.vector.memset(ln_step[:], math.log(STEP))
+        corner = held.tile([P, RUNGS], F32, name="corner")
+        nc.scalar.activation(corner[:], count[:], EXP, scale=STEP)
+        bend = held.tile([P, RUNGS], F32, name="bend")
+        nc.scalar.activation(bend[:, : RUNGS - 1], count[:, : RUNGS - 1], EXP, bias=ln_step[:], scale=-STEP)
+        nc.vector.memset(bend[:, RUNGS - 1 :], LAST_SLOPE)
 
         bags = [zeros, zeros]
         for t in range(T // 2):
@@ -86,17 +92,15 @@ def tile_gmemn2n_kernel(tc, wb, wout, offs, out):
             total = work.tile([P, 1], F32, name="total")
             nc.scalar.activation(powers[:], minus_z[:], EXP, bias=minus_peak[:], scale=-1.0, accum_out=total[:])
 
-            below = work.tile([P, RUNGS], F32, name="below")
-            rungs_below = work.tile([P, 1], F32, name="rungs_below")
-            nc.vector.tensor_scalar(
-                below[:], ladder[:], total[:], 0.5 - 1.0 / STEP, op0=IS_LE, op1=ADD, accum_out=rungs_below[:]
+            clipped = work.tile([P, RUNGS], F32, name="clipped")
+            line = work.tile([P, 1], F32, name="line")
+            nc.vector.scalar_tensor_tensor(
+                clipped[:], corner[:], total[:], bend[:], op0=MIN, op1=MULT, accum_out=line[:]
             )
-            shrink = work.tile([P, 1], F32, name="shrink")
-            nc.scalar.activation(shrink[:], rungs_below[:], EXP, bias=minus_one[:], scale=-STEP)
-            rest = work.tile([P, 1], F32, name="rest")
-            nc.vector.tensor_scalar(rest[:], rungs_below[:], STEP, minus_peak[:], op0=MULT, op1=SUBTRACT)
             log_sum_exp = work.tile([P, 1], F32, name="log_sum_exp")
-            nc.vector.tensor_scalar(log_sum_exp[:], shrink[:], total[:], rest[:], op0=MULT, op1=ADD)
+            nc.vector.tensor_scalar(
+                log_sum_exp[:], line[:], minus_peak[:], FIRST_SLOPE - SAG, op0=SUBTRACT, op1=SUBTRACT
+            )
 
             for h, (half, queue) in enumerate(((low, nc.sync), (high, nc.scalar))):
                 result = held.tile([P, BANK], F32, name=f"result{q}{h}")

@@ -6,7 +6,6 @@ F32 = mybir.dt.float32
 BF16 = mybir.dt.bfloat16
 U16 = mybir.dt.uint16
 ADD = mybir.AluOpType.add
-SUBTRACT = mybir.AluOpType.subtract
 MULT = mybir.AluOpType.mult
 MIN = mybir.AluOpType.min
 EXP = mybir.ActivationFunctionType.Exp
@@ -51,11 +50,16 @@ def tile_gmemn2n_kernel(tc, wb, wout, offs, out):
         nc.gpsimd.iota(count[:], [[1, RUNGS]], base=1, channel_multiplier=0, allow_small_or_imprecise_dtypes=True)
         ln_step = held.tile([P, 1], F32, name="ln_step")
         nc.vector.memset(ln_step[:], math.log(STEP))
-        corner = held.tile([P, RUNGS], F32, name="corner")
-        nc.scalar.activation(corner[:], count[:], EXP, scale=STEP)
-        bend = held.tile([P, RUNGS], F32, name="bend")
-        nc.scalar.activation(bend[:, : RUNGS - 1], count[:, : RUNGS - 1], EXP, bias=ln_step[:], scale=-STEP)
-        nc.vector.memset(bend[:, RUNGS - 1 :], LAST_SLOPE)
+        corner = held.tile([P, RUNGS + 2], F32, name="corner")
+        nc.scalar.activation(corner[:, :RUNGS], count[:], EXP, scale=STEP)
+        nc.vector.memset(corner[:, RUNGS:], -1.0)
+        bends = []
+        for q in blocks:
+            bend = held.tile([P, RUNGS + 2], F32, name=f"bend{q}")
+            nc.scalar.activation(bend[:, : RUNGS - 1], count[:, : RUNGS - 1], EXP, bias=ln_step[:], scale=-STEP)
+            nc.vector.memset(bend[:, RUNGS - 1 : RUNGS], LAST_SLOPE)
+            nc.vector.memset(bend[:, RUNGS : RUNGS + 1], FIRST_SLOPE - SAG)
+            bends.append(bend)
 
         bags = [zeros, zeros]
         for t in range(T // 2):
@@ -83,23 +87,19 @@ def tile_gmemn2n_kernel(tc, wb, wout, offs, out):
         for q in blocks:
             minus_z = work.tile([P, S], F32, name="minus_z")
             of_low = work.tile([P, 1], F32, name="of_low")
-            minus_peak = work.tile([P, 1], F32, name="minus_peak")
+            minus_peak = bends[q][:, RUNGS + 1 :]
             nc.vector.tensor_scalar(minus_z[:, low], z[q][:, low], -1.0, None, op0=MULT, op1=MIN, accum_out=of_low[:])
             nc.vector.tensor_scalar(
-                minus_z[:, high], z[q][:, high], -1.0, of_low[:], op0=MULT, op1=MIN, accum_out=minus_peak[:]
+                minus_z[:, high], z[q][:, high], -1.0, of_low[:], op0=MULT, op1=MIN, accum_out=minus_peak
             )
             powers = work.tile([P, S], BF16, name="powers")
             total = work.tile([P, 1], F32, name="total")
-            nc.scalar.activation(powers[:], minus_z[:], EXP, bias=minus_peak[:], scale=-1.0, accum_out=total[:])
+            nc.scalar.activation(powers[:], minus_z[:], EXP, bias=minus_peak, scale=-1.0, accum_out=total[:])
 
-            clipped = work.tile([P, RUNGS], F32, name="clipped")
-            line = work.tile([P, 1], F32, name="line")
-            nc.vector.scalar_tensor_tensor(
-                clipped[:], corner[:], total[:], bend[:], op0=MIN, op1=MULT, accum_out=line[:]
-            )
+            clipped = work.tile([P, RUNGS + 2], F32, name="clipped")
             log_sum_exp = work.tile([P, 1], F32, name="log_sum_exp")
-            nc.vector.tensor_scalar(
-                log_sum_exp[:], line[:], minus_peak[:], FIRST_SLOPE - SAG, op0=SUBTRACT, op1=SUBTRACT
+            nc.vector.scalar_tensor_tensor(
+                clipped[:], corner[:], total[:], bends[q][:], op0=MIN, op1=MULT, accum_out=log_sum_exp[:]
             )
 
             for h, (half, queue) in enumerate(((low, nc.sync), (high, nc.scalar))):

@@ -18,7 +18,7 @@ N = T * B
 P = 128
 BANK = 512
 PER_COLUMN = 16
-RUNGS = 256
+RUNGS = 128
 STEP = math.log(S) / RUNGS
 FIRST_SLOPE = STEP / (math.exp(STEP) - 1.0)
 LAST_SLOPE = FIRST_SLOPE * math.exp(-(RUNGS - 1) * STEP)

@@ -102,7 +102,7 @@ def tile_gmemn2n_kernel(tc, wb, wout, offs, out):
                 clipped[:], corner[:], total[:], bends[q][:], op0=MIN, op1=MULT, accum_out=log_sum_exp[:]
             )
 
-            for h, (half, queue) in enumerate(((low, nc.sync), (high, nc.scalar))):
+            for h, (half, queue) in enumerate(((low, nc.sync), (high, nc.sync))):
                 result = held.tile([P, BANK], F32, name=f"result{q}{h}")
                 nc.vector.tensor_scalar(result[:], minus_z[:, half], log_sum_exp[:], -1.0, op0=ADD, op1=MULT)
                 queue.dma_start(out[q * P : (q + 1) * P, half], result[:])

@@ -36,13 +36,12 @@ def tile_gmemn2n_kernel(tc, wb, wout, offs, out):
         tc.tile_pool(name="work", bufs=2) as work,
         tc.psum_pool(name="psum", bufs=1) as psum,
     ):
+        table = held.tile([C, S], F32, name="table")
+        nc.sync.dma_start(table[:], wb)
         offsets = held.tile([P, N // PER_COLUMN], U16, name="offsets")
         nc.sync.dma_start(offsets[:], offs)
-        table = held.tile([C, S], F32, name="table")
-        nc.scalar.dma_start(table[:, high], wb[:, high])
-        nc.sync.dma_start(table[:, low], wb[:, low])
         answers = held.tile([C, S], BF16, name="answers")
-        nc.scalar.dma_start(answers[:], wout)
+        nc.sync.dma_start(answers[:], wout)
         zeros = held.tile([C, B], F32, name="zeros")
         nc.vector.memset(zeros[:], 0.0)
 

@@ -7,6 +7,7 @@ BF16 = mybir.dt.bfloat16
 U16 = mybir.dt.uint16
 ADD = mybir.AluOpType.add
 MULT = mybir.AluOpType.mult
+MAX = mybir.AluOpType.max
 MIN = mybir.AluOpType.min
 EXP = mybir.ActivationFunctionType.Exp
 
@@ -18,11 +19,14 @@ N = T * B
 P = 128
 BANK = 512
 PER_COLUMN = 16
-RUNGS = 128
-STEP = math.log(S) / RUNGS
+CORNERS = 128
+STEP = math.log(S) / (CORNERS - 1)
 FIRST_SLOPE = STEP / (math.exp(STEP) - 1.0)
-LAST_SLOPE = FIRST_SLOPE * math.exp(-(RUNGS - 1) * STEP)
+LAST_SLOPE = FIRST_SLOPE * math.exp(-(CORNERS - 2) * STEP)
 SAG = STEP * STEP / 16.0
+STEEP = 1e35
+FENCE = 8
+RIGHT = FENCE + CORNERS
 
 FLOPS = 2 * B * C * S
 
@@ -45,20 +49,21 @@ def tile_gmemn2n_kernel(tc, wb, wout, offs, out):
         zeros = held.tile([C, B], F32, name="zeros")
         nc.vector.memset(zeros[:], 0.0)
 
-        count = held.tile([P, RUNGS], F32, name="count")
-        nc.gpsimd.iota(count[:], [[1, RUNGS]], base=1, channel_multiplier=0, allow_small_or_imprecise_dtypes=True)
-        ln_step = held.tile([P, 1], F32, name="ln_step")
-        nc.vector.memset(ln_step[:], math.log(STEP))
-        corner = held.tile([P, RUNGS + 2], F32, name="corner")
-        nc.scalar.activation(corner[:, :RUNGS], count[:], EXP, scale=STEP)
-        nc.vector.memset(corner[:, RUNGS:], -1.0)
-        bends = []
-        for q in blocks:
-            bend = held.tile([P, RUNGS + 2], F32, name=f"bend{q}")
-            nc.scalar.activation(bend[:, : RUNGS - 1], count[:, : RUNGS - 1], EXP, bias=ln_step[:], scale=-STEP)
-            nc.vector.memset(bend[:, RUNGS - 1 : RUNGS], LAST_SLOPE)
-            nc.vector.memset(bend[:, RUNGS : RUNGS + 1], FIRST_SLOPE - SAG)
-            bends.append(bend)
+        fall = held.tile([P, RIGHT + FENCE], F32, name="fall")
+        nc.gpsimd.memset(fall[:], -STEEP)
+        nc.gpsimd.memset(fall[:, FENCE : FENCE + 1], -STEP)
+        width = 1
+        while width < CORNERS:
+            done = fall[:, FENCE : FENCE + width]
+            more = fall[:, FENCE + width : FENCE + 2 * width]
+            nc.gpsimd.tensor_scalar(more, done, math.exp(-width * STEP), None, op0=MULT)
+            width *= 2
+        nc.gpsimd.memset(fall[:, FENCE : FENCE + 1], -STEEP)
+        nc.gpsimd.memset(fall[:, RIGHT - 1 : RIGHT], -LAST_SLOPE)
+        floor = held.tile([P, RIGHT + FENCE], F32, name="floor")
+        nc.gpsimd.memset(floor[:, FENCE:RIGHT], -STEP)
+        nc.gpsimd.memset(floor[:, FENCE : FENCE + 1], FIRST_SLOPE - SAG)
+        nc.gpsimd.memset(floor[:, RIGHT - 1 : RIGHT], -STEEP)
 
         bags = [zeros, zeros]
         for t in range(T // 2):
@@ -86,7 +91,8 @@ def tile_gmemn2n_kernel(tc, wb, wout, offs, out):
         for q in blocks:
             minus_z = work.tile([P, S], F32, name="minus_z")
             of_low = work.tile([P, 1], F32, name="of_low")
-            minus_peak = bends[q][:, RUNGS + 1 :]
+            own = slice(FENCE - 1 + q, RIGHT + q)
+            minus_peak = (floor[:, FENCE - 1 : FENCE], floor[:, RIGHT : RIGHT + 1])[q]
             nc.vector.tensor_scalar(minus_z[:, low], z[q][:, low], -1.0, None, op0=MULT, op1=MIN, accum_out=of_low[:])
             nc.vector.tensor_scalar(
                 minus_z[:, high], z[q][:, high], -1.0, of_low[:], op0=MULT, op1=MIN, accum_out=minus_peak
@@ -95,13 +101,13 @@ def tile_gmemn2n_kernel(tc, wb, wout, offs, out):
             total = work.tile([P, 1], F32, name="total")
             nc.scalar.activation(powers[:], minus_z[:], EXP, bias=minus_peak, scale=-1.0, accum_out=total[:])
 
-            clipped = work.tile([P, RUNGS + 2], F32, name="clipped")
-            log_sum_exp = work.tile([P, 1], F32, name="log_sum_exp")
+            terms = work.tile([P, CORNERS + 1], F32, name="terms")
+            minus_lse = work.tile([P, 1], F32, name="minus_lse")
             nc.vector.scalar_tensor_tensor(
-                clipped[:], corner[:], total[:], bends[q][:], op0=MIN, op1=MULT, accum_out=log_sum_exp[:]
+                terms[:], fall[:, own], total[:], floor[:, own], op0=MULT, op1=MAX, accum_out=minus_lse[:]
             )
 
             for h, (half, queue) in enumerate(((low, nc.sync), (high, nc.sync))):
                 result = held.tile([P, BANK], F32, name=f"result{q}{h}")
-                nc.vector.tensor_scalar(result[:], minus_z[:, half], log_sum_exp[:], -1.0, op0=ADD, op1=MULT)
+                nc.vector.tensor_scalar(result[:], minus_z[:, half], -1.0, minus_lse[:], op0=MULT, op1=ADD)
                 queue.dma_start(out[q * P : (q + 1) * P, half], result[:])

@@ -25,8 +25,7 @@ FIRST_SLOPE = STEP / (math.exp(STEP) - 1.0)
 LAST_SLOPE = FIRST_SLOPE * math.exp(-(CORNERS - 2) * STEP)
 SAG = STEP * STEP / 16.0
 STEEP = 1e35
-FENCE = 8
-RIGHT = FENCE + CORNERS
+RATIO = math.exp(-STEP)
 
 FLOPS = 2 * B * C * S
 
@@ -49,21 +48,16 @@ def tile_gmemn2n_kernel(tc, wb, wout, offs, out):
         zeros = held.tile([C, B], F32, name="zeros")
         nc.vector.memset(zeros[:], 0.0)
 
-        fall = held.tile([P, RIGHT + FENCE], F32, name="fall")
-        nc.gpsimd.memset(fall[:], -STEEP)
-        nc.gpsimd.memset(fall[:, FENCE : FENCE + 1], -STEP)
-        width = 1
-        while width < CORNERS:
-            done = fall[:, FENCE : FENCE + width]
-            more = fall[:, FENCE + width : FENCE + 2 * width]
-            nc.gpsimd.tensor_scalar(more, done, math.exp(-width * STEP), None, op0=MULT)
-            width *= 2
-        nc.gpsimd.memset(fall[:, FENCE : FENCE + 1], -STEEP)
-        nc.gpsimd.memset(fall[:, RIGHT - 1 : RIGHT], -LAST_SLOPE)
-        floor = held.tile([P, RIGHT + FENCE], F32, name="floor")
-        nc.gpsimd.memset(floor[:, FENCE:RIGHT], -STEP)
-        nc.gpsimd.memset(floor[:, FENCE : FENCE + 1], FIRST_SLOPE - SAG)
-        nc.gpsimd.memset(floor[:, RIGHT - 1 : RIGHT], -STEEP)
+        ratios = held.tile([P, CORNERS - 2], F32, name="ratios")
+        nc.vector.memset(ratios[:], RATIO)
+        fall = held.tile([P, CORNERS + 2], F32, name="fall")
+        nc.vector.memset(fall[:], -STEEP)
+        nc.vector.tensor_tensor_scan(fall[:, 2:CORNERS], ratios[:], zeros[:, : CORNERS - 2], -STEP, op0=MULT, op1=ADD)
+        nc.vector.memset(fall[:, CORNERS : CORNERS + 1], -LAST_SLOPE)
+        floor = held.tile([P, CORNERS + 2], F32, name="floor")
+        nc.vector.memset(floor[:], -STEP)
+        nc.vector.memset(floor[:, 1:2], FIRST_SLOPE - SAG)
+        nc.vector.memset(floor[:, CORNERS : CORNERS + 1], -STEEP)
 
         bags = [zeros, zeros]
         for t in range(T // 2):
@@ -83,19 +77,20 @@ def tile_gmemn2n_kernel(tc, wb, wout, offs, out):
                 nc.vector.tensor_tensor(longer[:], words, mine[t % 2], ADD)
                 mine[t % 2] = longer[:]
             u_bf = work.tile([C, P], BF16, name="u_bf")
-            nc.vector.tensor_tensor(u_bf[:], mine[0], mine[1], ADD)
-            z.append(psum.tile([P, S], F32, name=f"z{q}"))
-            for half in (low, high):
-                nc.tensor.matmul(z[q][:, half], u_bf[:], answers[:, half], start=True, stop=True)
+            adder = (nc.vector, nc.gpsimd)[q]
+            adder.tensor_tensor(u_bf[:], mine[0], mine[1], ADD)
+            z.append([psum.tile([P, BANK], F32, name=f"z{q}{h}") for h in range(2)])
+            for h, half in enumerate((low, high)):
+                nc.tensor.matmul(z[q][h][:], u_bf[:], answers[:, half], start=True, stop=True)
 
         for q in blocks:
             minus_z = work.tile([P, S], F32, name="minus_z")
             of_low = work.tile([P, 1], F32, name="of_low")
-            own = slice(FENCE - 1 + q, RIGHT + q)
-            minus_peak = (floor[:, FENCE - 1 : FENCE], floor[:, RIGHT : RIGHT + 1])[q]
-            nc.vector.tensor_scalar(minus_z[:, low], z[q][:, low], -1.0, None, op0=MULT, op1=MIN, accum_out=of_low[:])
+            own = slice(q, q + CORNERS + 1)
+            minus_peak = floor[:, q * (CORNERS + 1) : q * (CORNERS + 1) + 1]
+            nc.vector.tensor_scalar(minus_z[:, low], z[q][0][:], -1.0, None, op0=MULT, op1=MIN, accum_out=of_low[:])
             nc.vector.tensor_scalar(
-                minus_z[:, high], z[q][:, high], -1.0, of_low[:], op0=MULT, op1=MIN, accum_out=minus_peak
+                minus_z[:, high], z[q][1][:], -1.0, of_low[:], op0=MULT, op1=MIN, accum_out=minus_peak
             )
             powers = work.tile([P, S], BF16, name="powers")
             total = work.tile([P, 1], F32, name="total")

@@ -19,7 +19,7 @@ N = T * B
 P = 128
 BANK = 512
 PER_COLUMN = 16
-CORNERS = 128
+CORNERS = 96
 STEP = math.log(S) / (CORNERS - 1)
 FIRST_SLOPE = STEP / (math.exp(STEP) - 1.0)
 LAST_SLOPE = FIRST_SLOPE * math.exp(-(CORNERS - 2) * STEP)
@@ -102,7 +102,7 @@ def tile_gmemn2n_kernel(tc, wb, wout, offs, out):
                 terms[:], fall[:, own], total[:], floor[:, own], op0=MULT, op1=MAX, accum_out=minus_lse[:]
             )
 
-            for h, (half, queue) in enumerate(((low, nc.sync), (high, nc.sync))):
-                result = held.tile([P, BANK], F32, name=f"result{q}{h}")
-                nc.vector.tensor_scalar(result[:], minus_z[:, half], -1.0, minus_lse[:], op0=MULT, op1=ADD)
-                queue.dma_start(out[q * P : (q + 1) * P, half], result[:])
+            for i, piece in enumerate(((slice(0, S),), (low, high))[q]):
+                result = held.tile([P, S // (q + 1)], F32, name=f"result{q}{i}")
+                nc.vector.tensor_scalar(result[:], minus_z[:, piece], -1.0, minus_lse[:], op0=MULT, op1=ADD)
+                nc.sync.dma_start(out[q * P : (q + 1) * P, piece], result[:])

@@ -102,7 +102,8 @@ def tile_gmemn2n_kernel(tc, wb, wout, offs, out):
                 terms[:], fall[:, own], total[:], floor[:, own], op0=MULT, op1=MAX, accum_out=minus_lse[:]
             )
 
-            for i, piece in enumerate(((slice(0, S),), (low, high))[q]):
-                result = held.tile([P, S // (q + 1)], F32, name=f"result{q}{i}")
+            for i, piece in enumerate(((slice(0, S),), (slice(0, S // 4), slice(S // 4, S)))[q]):
+                width = piece.stop - piece.start
+                result = held.tile([P, width], F32, name=f"result{q}{i}")
                 nc.vector.tensor_scalar(result[:], minus_z[:, piece], -1.0, minus_lse[:], op0=MULT, op1=ADD)
                 nc.sync.dma_start(out[q * P : (q + 1) * P, piece], result[:])

import math

import concourse.mybir as mybir

F32 = mybir.dt.float32
BF16 = mybir.dt.bfloat16
U16 = mybir.dt.uint16
ADD = mybir.AluOpType.add
MULT = mybir.AluOpType.mult
MAX = mybir.AluOpType.max
MIN = mybir.AluOpType.min
EXP = mybir.ActivationFunctionType.Exp

C = 128
S = 1024
B = 256
T = 8
N = T * B
P = 128
BANK = 512
PER_COLUMN = 16
CORNERS = 96
STEP = math.log(S) / (CORNERS - 1)
FIRST_SLOPE = STEP / (math.exp(STEP) - 1.0)
LAST_SLOPE = FIRST_SLOPE * math.exp(-(CORNERS - 2) * STEP)
SAG = STEP * STEP / 16.0
STEEP = 1e35
RATIO = math.exp(-STEP)

FLOPS = 2 * B * C * S


def tile_gmemn2n_kernel(tc, wb, wout, offs, out):
    nc = tc.nc
    low, high = slice(0, BANK), slice(BANK, S)
    blocks = range(B // P)
    with (
        tc.tile_pool(name="held", bufs=1) as held,
        tc.tile_pool(name="work", bufs=2) as work,
        tc.psum_pool(name="psum", bufs=1) as psum,
    ):
        table = held.tile([C, S], F32, name="table")
        nc.sync.dma_start(table[:], wb)
        offsets = held.tile([P, N // PER_COLUMN], U16, name="offsets")
        nc.sync.dma_start(offsets[:], offs)
        answers = held.tile([C, S], BF16, name="answers")
        nc.sync.dma_start(answers[:], wout)
        zeros = held.tile([C, B], F32, name="zeros")
        nc.vector.memset(zeros[:], 0.0)

        ratios = held.tile([P, CORNERS - 2], F32, name="ratios")
        nc.vector.memset(ratios[:], RATIO)
        fall = held.tile([P, CORNERS + 2], F32, name="fall")
        nc.vector.memset(fall[:], -STEEP)
        nc.vector.tensor_tensor_scan(fall[:, 2:CORNERS], ratios[:], zeros[:, : CORNERS - 2], -STEP, op0=MULT, op1=ADD)
        nc.vector.memset(fall[:, CORNERS : CORNERS + 1], -LAST_SLOPE)
        floor = held.tile([P, CORNERS + 2], F32, name="floor")
        nc.vector.memset(floor[:], -STEP)
        nc.vector.memset(floor[:, 1:2], FIRST_SLOPE - SAG)
        nc.vector.memset(floor[:, CORNERS : CORNERS + 1], -STEEP)

        bags = [zeros, zeros]
        for t in range(T // 2):
            words = table[:].indirect(offsets[:, t * B // PER_COLUMN : (t + 1) * B // PER_COLUMN])
            longer = work.tile([C, B], F32, name=f"bag{t % 2}")
            nc.vector.tensor_tensor(longer[:], words, bags[t % 2][:], ADD)
            bags[t % 2] = longer

        z = []
        for q in blocks:
            asked = slice(q * P, (q + 1) * P)
            mine = [bags[0][:, asked], bags[1][:, asked]]
            for t in range(T // 2, T):
                first = (t * B + q * P) // PER_COLUMN
                words = table[:].indirect(offsets[:, first : first + P // PER_COLUMN])
                longer = work.tile([C, P], F32, name=f"mine{t % 2}")
                nc.vector.tensor_tensor(longer[:], words, mine[t % 2], ADD)
                mine[t % 2] = longer[:]
            u_bf = work.tile([C, P], BF16, name="u_bf")
            adder = (nc.vector, nc.gpsimd)[q]
            adder.tensor_tensor(u_bf[:], mine[0], mine[1], ADD)
            z.append([psum.tile([P, BANK], F32, name=f"z{q}{h}") for h in range(2)])
            for h, half in enumerate((low, high)):
                nc.tensor.matmul(z[q][h][:], u_bf[:], answers[:, half], start=True, stop=True)

        for q in blocks:
            minus_z = work.tile([P, S], F32, name="minus_z")
            of_low = work.tile([P, 1], F32, name="of_low")
            own = slice(q, q + CORNERS + 1)
            minus_peak = floor[:, q * (CORNERS + 1) : q * (CORNERS + 1) + 1]
            nc.vector.tensor_scalar(minus_z[:, low], z[q][0][:], -1.0, None, op0=MULT, op1=MIN, accum_out=of_low[:])
            nc.vector.tensor_scalar(
                minus_z[:, high], z[q][1][:], -1.0, of_low[:], op0=MULT, op1=MIN, accum_out=minus_peak
            )
            powers = work.tile([P, S], BF16, name="powers")
            total = work.tile([P, 1], F32, name="total")
            nc.scalar.activation(powers[:], minus_z[:], EXP, bias=minus_peak, scale=-1.0, accum_out=total[:])

            terms = work.tile([P, CORNERS + 1], F32, name="terms")
            minus_lse = work.tile([P, 1], F32, name="minus_lse")
            nc.vector.scalar_tensor_tensor(
                terms[:], fall[:, own], total[:], floor[:, own], op0=MULT, op1=MAX, accum_out=minus_lse[:]
            )

            for i, piece in enumerate(((slice(0, S),), (slice(0, S // 4), slice(S // 4, S)))[q]):
                width = piece.stop - piece.start
                result = held.tile([P, width], F32, name=f"result{q}{i}")
                nc.vector.tensor_scalar(result[:], minus_z[:, piece], -1.0, minus_lse[:], op0=MULT, op1=ADD)
                nc.sync.dma_start(out[q * P : (q + 1) * P, piece], result[:])
